import numpy as np
import ml_dtypes


def mxq(x, axis, fmt="e4m3"):
    dtype, down = {"e4m3": (ml_dtypes.float8_e4m3fn, 7), "e5m2": (ml_dtypes.float8_e5m2, 14)}[fmt]
    v = np.moveaxis(np.asarray(x, np.float32).astype(ml_dtypes.bfloat16).astype(np.float64), axis, -1)
    blocks = v.reshape(v.shape[:-1] + (-1, 32))
    amax = np.abs(blocks).max(-1, keepdims=True)
    byte = np.maximum(np.where(amax > 0, np.frexp(amax)[1] - 1 + 127, 0) - down, 1)
    scale = np.exp2(byte - 127.0)
    codes = (blocks / scale).astype(np.float32).astype(dtype).astype(np.float64)
    return np.moveaxis((codes * scale).reshape(v.shape), -1, axis)


WIDE = False


def mx_kscale(k):
    if not WIDE:
        return np.ones(k)
    levels = np.array([30, -30])
    if k % 512:
        return np.exp2(np.random.permutation(np.resize(levels, k // 32))).repeat(32)
    a = np.empty((k // 512, 16))
    for p in range(k // 512):
        a[p, :8] = np.random.permutation(np.resize(levels, 8))
        for g in range(8):
            far = levels[np.abs(levels - a[p, g]) >= 10]
            a[p, g + 8] = far[np.random.randint(len(far))]
    return np.exp2(a.ravel()).repeat(32)


BF16 = ml_dtypes.bfloat16


def bf(x):
    return np.asarray(x, np.float32).astype(BF16)


def f64(x):
    return np.asarray(x).astype(np.float64)


B, I, H = 2048, 512, 256
EPS = 1e-5


def sigmoid(v):
    return 1.0 / (1.0 + np.exp(-v))


def _bn(v, gamma, beta):
    m = np.mean(v, axis=0)
    var = np.var(v, axis=0)
    return (v - m) * (gamma / np.sqrt(var + EPS)) + beta


def setup_inputs():
    rn = np.random.standard_normal
    s = mx_kscale(I)
    return {"x": bf(rn((B, I)) * s),
            "c": bf(rn((B, H))),
            "h": bf(rn((B, H))),
            "w_ih": bf(rn((4 * H, I)) / np.sqrt(I) / s),
            "w_hh": bf(rn((4 * H, H)) / np.sqrt(H)),
            "b": bf(0.3 * rn(4 * H)),
            "g_ih": bf(1.0 + 0.1 * rn(4 * H)),
            "b_ih": bf(0.3 * rn(4 * H)),
            "g_hh": bf(1.0 + 0.1 * rn(4 * H)),
            "b_hh": bf(0.3 * rn(4 * H)),
            "g_c": bf(1.0 + 0.1 * rn(H)),
            "b_c": bf(0.3 * rn(H))}


def reference(x, c, h, w_ih, w_hh, b, g_ih, b_ih, g_hh, b_hh, g_c, b_c):
    ih = mxq(f64(x), 1, "e5m2") @ mxq(f64(w_ih), 1, "e5m2").T
    hh = f64(h) @ f64(w_hh).T
    ih = _bn(ih, f64(g_ih), f64(b_ih))
    hh = _bn(hh, f64(g_hh), f64(b_hh))
    gates = ih + hh + f64(b)
    f, i, o, g = np.split(gates, 4, axis=1)
    f = sigmoid(f)
    i = sigmoid(i)
    o = sigmoid(o)
    g = np.tanh(g)
    c_next = f * f64(c) + i * g
    c_next = _bn(c_next, f64(g_c), f64(b_c))
    h_next = o * np.tanh(c_next)
    return (c_next, h_next)

@@ -1,0 +1,598 @@
+from contextlib import ExitStack
+
+import concourse.mybir as mybir
+from concourse.masks import make_identity
+
+B, I, H = 2048, 512, 256
+EPS = 1e-5
+FLOPS = 2 * B * 4 * H * (I + H)
+
+F32 = mybir.dt.float32
+BF16 = mybir.dt.bfloat16
+U32 = mybir.dt.uint32
+U8 = mybir.dt.uint8
+E5M2X4 = mybir.dt.float8_e5m2_x4
+ALU = mybir.AluOpType
+ACT = mybir.ActivationFunctionType
+
+P = 128
+ROWS = B // P
+CHUNK = 512
+CHUNKS = B // CHUNK
+RPC = CHUNK // P
+F, IN, O, G = 0, 1, 2, 3
+TILES = [(IN, 0), (G, 0), (F, 0), (IN, 1), (G, 1), (F, 1), (O, 0), (O, 1)]
+TINY = 2.0**-60
+BANKS = 4
+LEAD = 2
+VECTOR_VAR = (0, 3)
+
+
+def tile_lstmcell_kernel(
+    tc, x, c, h, w_ih, w_hh, b, g_ih, b_ih, g_hh, b_hh, g_c, b_c, out_0, out_1
+):
+    nc = tc.nc
+    with ExitStack() as ctx:
+        sb = ctx.enter_context(tc.tile_pool(name="sb", bufs=1))
+        ps = ctx.enter_context(tc.psum_pool(name="ps", bufs=1))
+        ctx.enter_context(tc.manual_schedule())
+
+        def bank(n, shape, dtype):
+            return ps.tile([P] + shape, dtype, name="bank%d" % n, tag="bank%d" % n)
+
+        def tile(name, shape, dtype):
+            return sb.tile([P] + shape, dtype, name=name, align_bytes=64)
+
+        def tiles(name, count, shape, dtype):
+            return [tile("%s%d" % (name, n), shape, dtype) for n in range(count)]
+
+        x_rows = tiles("x_rows", CHUNKS, [RPC, I], BF16)
+        h_rows = tiles("h_rows", CHUNKS, [RPC, H], BF16)
+        c_rows = tile("c_rows", [ROWS, H], BF16)
+        wih_rows = tiles("wih_rows", 2, [4, I], BF16)
+        whh_rows = tiles("whh_rows", 2, [4, H], BF16)
+        x_k = tiles("x_k", CHUNKS, [CHUNK, 4], BF16)
+        x_codes = tiles("x_codes", CHUNKS, [CHUNK], U32)
+        x_scales = tiles("x_scales", CHUNKS, [CHUNK], U8)
+        wih_k = tiles("wih_k", 2, [4 * P, 4], BF16)
+        wih_codes = tiles("wih_codes", 2, [4 * P], U32)
+        wih_scales = tiles("wih_scales", 2, [4 * P], U8)
+        h_t = tiles("h_t", CHUNKS, [2, CHUNK], BF16)
+        whh_t = tiles("whh_t", 2, [4, 2, P], BF16)
+        gate = tiles("gate", 8, [B], F32)
+        squares = tile("squares", [B], BF16)
+        c_out = tiles("c_out", 2 * CHUNKS, [RPC, P], F32)
+        tanh_c = tiles("tanh_c", 2 * CHUNKS, [RPC, P], F32)
+        h_out = tiles("h_out", CHUNKS, [RPC, H], F32)
+        ident_f = tile("ident_f", [P], F32)
+        ident_b = tile("ident_b", [P], BF16)
+        vec_rows = tile("vec_rows", [P], BF16)
+        vec = tile("vec", [44], F32)
+        powers = tile("powers", [3], F32)
+        bias_sum = tile("bias_sum", [8], F32)
+        nudge = tile("nudge", [8], F32)
+        ghh_pm = tile("ghh_pm", [2, 8], F32)
+        gc_pm = tile("gc_pm", [2, 2], F32)
+        ghh_inv = tile("ghh_inv", [8], F32)
+        g_ratio = tile("g_ratio", [8], F32)
+        hh_sums = tile("hh_sums", [8, CHUNKS], F32)
+        hh_parts = tile("hh_parts", [8, CHUNKS], F32)
+        hh_stats = tile("hh_stats", [8, CHUNKS, 6], F32)
+        hh_mv = tile("hh_mv", [8, 2], F32)
+        var_eps = tile("var_eps", [8, 3], F32)
+        roots = tile("roots", [8, 3], F32)
+        sum_mean = tile("sum_mean", [8], F32)
+        hh_scale = tile("hh_scale", [8, 2], F32)
+        ih_stats = tile("ih_stats", [8, CHUNKS, 6], F32)
+        ih_mv = tile("ih_mv", [8, 2], F32)
+        ratio = tile("ratio", [8], F32)
+        gate_bias = tile("gate_bias", [8], F32)
+        c_stats = tile("c_stats", [2, CHUNKS, 6], F32)
+        c_mv = tile("c_mv", [2, 2], F32)
+        c_scale = tile("c_scale", [2, 2], F32)
+        c_rstd = tile("c_rstd", [2], F32)
+        c_bias = tile("c_bias", [2], F32)
+
+        x_v = x.rearrange("(p r) k -> p r k", r=ROWS)
+        h_v = h.rearrange("(p r) k -> p r k", r=ROWS)
+        c_v = c.rearrange("(p r) k -> p r k", r=ROWS)
+        wih_v = w_ih.rearrange("(g u m) k -> u m g k", g=4, u=2)
+        whh_v = w_hh.rearrange("(g u m) k -> u m g k", g=4, u=2)
+        c_next_v = out_0.rearrange("(p r) f -> p r f", r=ROWS)
+        h_next_v = out_1.rearrange("(p r) f -> p r f", r=ROWS)
+
+        def cols(k, n=1):
+            return slice(k * CHUNK, (k + n) * CHUNK)
+
+        def rows(k):
+            return slice(k * RPC, (k + 1) * RPC)
+
+        def pool_tt(out, in0, in1, op):
+            nc.gpsimd.tensor_tensor(out=out, in0=in0, in1=in1, op=op)
+
+        def pool_affine(out, in0, scale, bias):
+            nc.gpsimd.tensor_scalar(out, in0, scale, bias, ALU.mult, ALU.add)
+
+        def pool_product(out, in0, a, b):
+            nc.gpsimd.tensor_scalar(out, in0, a, b, ALU.mult, ALU.mult)
+
+        def column(t):
+            return 2 * TILES[t][0] + TILES[t][1]
+
+        def one(t):
+            return slice(t, t + 1)
+
+        nc.sync.dma_start(out=whh_rows[0][:], in_=whh_v[0])
+        for k in range(CHUNKS):
+            nc.sync.dma_start(out=h_rows[k][:], in_=h_v[:, rows(k), :])
+        nc.sync.dma_start(out=wih_rows[0][:], in_=wih_v[0])
+        for k in range(CHUNKS):
+            nc.sync.dma_start(out=x_rows[k][:], in_=x_v[:, rows(k), :])
+        nc.sync.dma_start(out=whh_rows[1][:], in_=whh_v[1])
+        nc.sync.dma_start(out=wih_rows[1][:], in_=wih_v[1])
+        nc.sync.dma_start(out=c_rows[:], in_=c_v)
+
+        make_identity(nc, ident_f[:])
+        nc.scalar.activation(out=ident_b[:], in_=ident_f[:], func=ACT.Identity)
+        nc.vector.memset(vec_rows[:], 0.0)
+        nc.vector.memset(powers[:, 0:1], 0.5)
+        nc.vector.memset(powers[:, 1:3], -0.5)
+        row = 0
+        for v in (g_hh, g_ih, b, b_ih, b_hh, g_c, b_c):
+            count = v.shape[0] // P
+            nc.gpsimd.dma_start(
+                out=vec_rows[row : row + count, :], in_=v.rearrange("(t m) -> t m", m=P)
+            )
+            row += count
+
+        def vectors():
+            def fill(n):
+                t = bank(n, [P], BF16)
+                nc.tensor.transpose(t[:], vec_rows[:], ident_b[:])
+                return t
+
+            def read(t):
+                nc.vector.tensor_copy(out=vec[:], in_=t[:, 0:44])
+                pool_tt(nudge[:], vec[:, 0:8], vec[:, 0:8], ALU.mult)
+                nc.gpsimd.tensor_scalar(
+                    nudge[:], nudge[:], TINY * TINY, 2 * TINY, ALU.is_lt, ALU.mult
+                )
+                pool_tt(ghh_pm[:, 0, :], vec[:, 0:8], nudge[:], ALU.add)
+                pool_affine(ghh_pm[:, 1, :], ghh_pm[:, 0, :], -1.0, 0.0)
+                pool_affine(gc_pm[:, 0, :], vec[:, 40:42], 1.0, 0.0)
+                pool_affine(gc_pm[:, 1, :], vec[:, 40:42], -1.0, 0.0)
+                pool_tt(bias_sum[:], vec[:, 16:24], vec[:, 24:32], ALU.add)
+                pool_tt(bias_sum[:], bias_sum[:], vec[:, 32:40], ALU.add)
+
+            return fill, read
+
+        def gain_ratio():
+            def read(t):
+                nc.vector.reciprocal(out=ghh_inv[:], in_=ghh_pm[:, 0, :])
+                pool_tt(g_ratio[:], vec[:, 8:16], ghh_inv[:], ALU.mult)
+
+            return None, read
+
+        def turn_whh(u, copy):
+            def fill(n):
+                t = bank(n, [4, 2, P], BF16)
+                for g in range(4):
+                    for kc in range(2):
+                        nc.tensor.transpose(
+                            t[:, g, kc, :], whh_rows[u][:, g, kc * P : (kc + 1) * P], ident_b[:]
+                        )
+                return t
+
+            return fill, lambda t: copy(out=whh_t[u][:], in_=t[:])
+
+        def turn_h(k, copy):
+            def fill(n):
+                t = bank(n, [2, RPC, P], BF16)
+                for kc in range(2):
+                    for j in range(RPC):
+                        nc.tensor.transpose(
+                            t[:, kc, j, :], h_rows[k][:, j, kc * P : (kc + 1) * P], ident_b[:]
+                        )
+                return t
+
+            return fill, lambda t: copy(out=h_t[k][:], in_=t[:].rearrange("p a j n -> p a (j n)"))
+
+        def turn_words(src, dst, pair, copy):
+            def fill(n):
+                words = src[:].bitcast(F32)
+                t = bank(n, [2, 2, P], F32)
+                for j in range(2):
+                    for w in range(2):
+                        nc.tensor.transpose(
+                            t[:, j, w, :], words[:, 2 * pair + j, w : I // 2 : 2], ident_f[:]
+                        )
+                return t
+
+            def read(t):
+                out = dst[:, 2 * pair * P : 2 * (pair + 1) * P, :].bitcast(F32)
+                copy(
+                    out=out.rearrange("p (j n) w -> p j n w", j=2),
+                    in_=t[:].rearrange("p j w n -> p j n w"),
+                )
+
+            return fill, read
+
+        def turn_x(k, pair, copy):
+            return turn_words(x_rows[k], x_k[k], pair, copy)
+
+        def turn_wih(u, pair, copy):
+            return turn_words(wih_rows[u], wih_k[u], pair, copy)
+
+        def quantize(src, codes, scales):
+            def read(t):
+                nc.vector.quantize_mx(
+                    out=codes[:].bitcast(E5M2X4),
+                    scales=scales[:],
+                    in_=src[:].rearrange("p n j -> p (n j)"),
+                )
+
+            return None, read
+
+        def quantize_x(k):
+            return quantize(x_k[k], x_codes[k], x_scales[k])
+
+        def quantize_wih(u):
+            return quantize(wih_k[u], wih_codes[u], wih_scales[u])
+
+        def hh(t, k):
+            g, u = TILES[t]
+
+            def fill(n):
+                acc = bank(n, [CHUNK], F32)
+                for kc in range(2):
+                    nc.tensor.matmul(
+                        out=acc[:],
+                        lhsT=whh_t[u][:, g, kc, :],
+                        rhs=h_t[k][:, kc, :],
+                        start=(kc == 0),
+                        stop=(kc == 1),
+                    )
+                return acc
+
+            def read(acc):
+                nc.scalar.activation(
+                    out=gate[t][:, cols(k)],
+                    in_=acc[:],
+                    func=ACT.Identity,
+                    accum_out=hh_sums[:, t, k : k + 1],
+                )
+
+            def read_plain(acc):
+                nc.scalar.copy(out=gate[t][:, cols(k)], in_=acc[:])
+
+            return fill, read_plain if t in VECTOR_VAR else read
+
+        def hh_stat(t, k):
+            def read(unused):
+                nc.vector.bn_stats(out=hh_stats[:, t, k, :], in_=gate[t][:, cols(k)])
+
+            return None, read
+
+        def hh_aggr(t):
+            def read(unused):
+                nc.vector.bn_aggr(
+                    out=hh_mv[:, t, :], in_=hh_stats[:, t, :, :].rearrange("p k s -> p (k s)")
+                )
+
+            return None, read
+
+        def hh_mean(t):
+            def read(unused):
+                nc.scalar.activation(
+                    out=hh_parts[:, t, :],
+                    in_=hh_sums[:, t, :],
+                    func=ACT.Identity,
+                    scale=1.0 / B,
+                    accum_out=hh_mv[:, t, 0:1],
+                )
+
+            return None, read
+
+        def hh_square(t):
+            def read(unused):
+                nc.scalar.activation(
+                    out=squares[:],
+                    in_=gate[t][:],
+                    func=ACT.Square,
+                    scale=-1.0,
+                    bias=hh_mv[:, t, 0:1],
+                    accum_out=hh_mv[:, t, 1:2],
+                )
+
+            return None, read
+
+        def ih_fill(t, k):
+            g, u = TILES[t]
+
+            def fill(n):
+                acc = bank(n, [CHUNK], F32)
+                nc.tensor.matmul_mx(
+                    out=acc[:],
+                    lhsT=wih_codes[u][:, g * P : (g + 1) * P].bitcast(E5M2X4),
+                    lhsT_scale=wih_scales[u][:, g * P : (g + 1) * P],
+                    rhs=x_codes[k][:].bitcast(E5M2X4),
+                    rhs_scale=x_scales[k][:],
+                    start=True,
+                    stop=True,
+                )
+                return acc
+
+            return fill
+
+        def ih_stat(t, k):
+            def read(acc):
+                nc.vector.bn_stats(out=ih_stats[:, t, k, :], in_=acc[:])
+
+            return ih_fill(t, k), read
+
+        def ih_aggr(t):
+            def read(unused):
+                nc.vector.bn_aggr(
+                    out=ih_mv[:, t, :], in_=ih_stats[:, t, :, :].rearrange("p k s -> p (k s)")
+                )
+
+            return None, read
+
+        def gate_scales(t):
+            factor = 1.0 if t in VECTOR_VAR else 1.0 / B
+            pool_affine(var_eps[:, t, 0:2], hh_mv[:, t, 1:2].to_broadcast([P, 2]), factor, EPS)
+            pool_affine(var_eps[:, t, 2:3], ih_mv[:, t, 1:2], 1.0, EPS)
+            pool_tt(roots[:, t, :], var_eps[:, t, :], powers[:], ALU.pow)
+            pool_product(
+                ratio[:, one(t)], roots[:, t, 0:1], roots[:, t, 2:3], g_ratio[:, one(column(t))]
+            )
+            pool_product(hh_scale[:, t, :], ghh_pm[:, :, column(t)], roots[:, t, 1:2], 1.0)
+
+        def mean_of_sum(t):
+            def read(unused):
+                nc.scalar.activation(
+                    out=sum_mean[:, one(t)],
+                    in_=ih_mv[:, t, 0:1],
+                    func=ACT.Identity,
+                    scale=ratio[:, one(t)],
+                    bias=hh_mv[:, t, 0:1],
+                )
+
+            return None, read
+
+        def bias_of_gate(t):
+            def read(unused):
+                nc.scalar.activation(
+                    out=gate_bias[:, one(t)],
+                    in_=sum_mean[:, one(t)],
+                    func=ACT.Identity,
+                    scale=hh_scale[:, t, 1:2],
+                    bias=bias_sum[:, one(column(t))],
+                )
+
+            return None, read
+
+        def join(t, k):
+            def read(acc):
+                nc.vector.scalar_tensor_tensor(
+                    out=gate[t][:, cols(k)],
+                    in0=acc[:],
+                    scalar=ratio[:, t : t + 1],
+                    in1=gate[t][:, cols(k)],
+                    op0=ALU.mult,
+                    op1=ALU.add,
+                )
+
+            return ih_fill(t, k), read
+
+        def activate(t, k, n=1):
+            g, u = TILES[t]
+
+            def read(unused):
+                nc.scalar.activation(
+                    out=gate[t][:, cols(k, n)],
+                    in_=gate[t][:, cols(k, n)],
+                    func=ACT.Tanh if g == G else ACT.Sigmoid,
+                    scale=hh_scale[:, t, 0:1],
+                    bias=gate_bias[:, t : t + 1],
+                )
+
+            return None, read
+
+        def forget(u, half):
+            def fill(n):
+                t = bank(n, [2 * RPC, P], BF16)
+                for j in range(2 * RPC):
+                    r = 2 * half * RPC + j
+                    nc.tensor.transpose(t[:, j, :], c_rows[:, r, u * P : (u + 1) * P], ident_b[:])
+                return t
+
+            def read(t):
+                f = gate[3 * u + 2][:, cols(2 * half, 2)]
+                nc.vector.tensor_tensor(
+                    out=f, in0=t[:].rearrange("p j n -> p (j n)"), in1=f, op=ALU.mult
+                )
+
+            return fill, read
+
+        def c_stat(u, k):
+            def read(unused):
+                nc.vector.bn_stats(out=c_stats[:, u, k, :], in_=gate[3 * u][:, cols(k)])
+
+            return None, read
+
+        def c_aggr(u):
+            def read(unused):
+                nc.vector.bn_aggr(
+                    out=c_mv[:, u, :], in_=c_stats[:, u, :, :].rearrange("p k s -> p (k s)")
+                )
+
+            return None, read
+
+        def c_small(u):
+            r, bias = c_rstd[:, one(u)], c_bias[:, one(u)]
+            pool_affine(r, c_mv[:, u, 1:2], 1.0, EPS)
+            pool_tt(r, r, powers[:, 1:2], ALU.pow)
+            pool_product(c_scale[:, u, :], gc_pm[:, :, u], r, 1.0)
+            pool_affine(bias, c_mv[:, u, 0:1], c_scale[:, u, 1:2], vec[:, one(42 + u)])
+
+        def input_gate(u, k):
+            cell = gate[3 * u][:, cols(k)]
+            pool_tt(cell, cell, gate[3 * u + 1][:, cols(k)], ALU.mult)
+
+        def cell_sum(u, k):
+            cell = gate[3 * u][:, cols(k)]
+            pool_tt(cell, cell, gate[3 * u + 2][:, cols(k)], ALU.add)
+
+        def c_norm(u, k):
+            cell = gate[3 * u][:, cols(k)]
+            pool_affine(cell, cell, c_scale[:, u, 0:1], c_bias[:, one(u)])
+
+        def pool(work, *args):
+            return None, lambda unused: work(*args)
+
+        def turn_back(src, k):
+            def fill(n):
+                t = bank(n, [RPC, P], F32)
+                for j in range(RPC):
+                    r = k * RPC + j
+                    nc.tensor.transpose(t[:, j, :], src[:, r * P : (r + 1) * P], ident_f[:])
+                return t
+
+            return fill
+
+        def c_finish(u, k):
+            m = u * CHUNKS + k
+
+            def read(t):
+                nc.scalar.activation(out=tanh_c[m][:], in_=t[:], func=ACT.Tanh)
+                nc.scalar.copy(out=c_out[m][:], in_=t[:])
+                nc.sync.dma_start(out=c_next_v[:, rows(k), u * P : (u + 1) * P], in_=c_out[m][:])
+
+            return turn_back(gate[3 * u], k), read
+
+        def h_finish(u, k):
+            m = u * CHUNKS + k
+
+            def read(t):
+                nc.vector.tensor_tensor(
+                    out=h_out[k][:, :, u * P : (u + 1) * P],
+                    in0=t[:],
+                    in1=tanh_c[m][:],
+                    op=ALU.mult,
+                )
+                if u == 1:
+                    nc.sync.dma_start(out=h_next_v[:, rows(k), :], in_=h_out[k][:])
+
+            return turn_back(gate[6 + u], k), read
+
+        def chunks(step, *args):
+            return [step(*args, k) for k in range(CHUNKS)]
+
+        def weave(*lists):
+            return [s for group in zip(*lists) for s in group]
+
+        def then(step, *more):
+            def read(t):
+                step[1](t)
+                for extra in more:
+                    extra[1](None)
+
+            return step[0], read
+
+        def after_first(steps, *more):
+            return [then(steps[0], *more)] + steps[1:]
+
+        REST = (None, None)
+        v_copy, s_copy = nc.vector.tensor_copy, nc.scalar.copy
+
+
+        def pairs(t):
+            return [activate(t, 0, 2), REST, activate(t, 2, 2), REST]
+
+        def square(t):
+            return [hh_square(t), REST, REST, REST]
+
+        def ih_done(t):
+            return then(ih_aggr(t), pool(gate_scales, t))
+
+        def pools(work, u, ks):
+            return [pool(work, u, k) for k in ks]
+
+        def hh_with_bias(t, earlier):
+            steps = chunks(hh, t)
+            return [then(steps[0], mean_of_sum(earlier)), then(steps[1], bias_of_gate(earlier))] + steps[2:]
+
+        def tanh_pairs(u):
+            t = 3 * u + 1
+            return [then(activate(t, 0, 2), *pools(input_gate, u, (0, 1))), REST, then(activate(t, 2, 2), *pools(input_gate, u, (2, 3))), REST]
+
+        head_vector = [
+            turn_whh(0, v_copy), turn_h(0, v_copy), turn_h(1, v_copy), turn_h(2, v_copy), turn_h(3, v_copy),
+            REST, turn_wih(0, 0, v_copy), hh_stat(0, 0), vectors(), quantize_wih(0),
+            turn_x(0, 0, v_copy), then(hh_stat(0, 1), gain_ratio()), quantize_x(0),
+            turn_x(1, 0, v_copy), hh_stat(0, 2), quantize_x(1),
+            turn_x(2, 0, v_copy), hh_stat(0, 3), quantize_x(2),
+            then(turn_x(3, 0, v_copy), hh_aggr(0)), ih_stat(0, 0), quantize_x(3),
+            ih_stat(0, 1), ih_stat(0, 2), ih_stat(0, 3),
+        ] + after_first(chunks(ih_stat, 1), ih_done(0))
+        head_scalar = [
+            REST, REST, REST, REST, hh(0, 0),
+            hh(0, 1), turn_wih(0, 1, s_copy), hh(0, 2), hh(0, 3), hh(1, 0),
+            turn_x(0, 1, s_copy), hh(1, 1), REST,
+            turn_x(1, 1, s_copy), hh(1, 2), REST,
+            turn_x(2, 1, s_copy), hh(1, 3), REST,
+            then(turn_x(3, 1, s_copy), hh_mean(1)), REST] + square(1) + chunks(hh, 2)
+        phases = [
+            (head_vector, head_scalar),
+            (
+                after_first(chunks(join, 0), ih_done(1)) + chunks(ih_stat, 2) + after_first(chunks(join, 1), ih_done(2)),
+                [then(turn_whh(1, s_copy), hh_mean(2), mean_of_sum(0))] + after_first(square(2), bias_of_gate(0))
+                + [then(activate(0, 0, 2), mean_of_sum(1)), REST, then(activate(0, 2, 2), bias_of_gate(1)), REST] + chunks(hh, 3)[:3],
+            ),
+            (
+                [turn_wih(1, 0, v_copy), turn_wih(1, 1, v_copy), join(2, 0), quantize_wih(1)] + chunks(join, 2)[1:]
+                + chunks(ih_stat, 3) + [hh_stat(3, 0)],
+                [hh(3, 3)] + tanh_pairs(0) + hh_with_bias(4, 2) + after_first(pairs(2), hh_mean(4))[:3],
+            ),
+            (
+                after_first(chunks(hh_stat, 3)[1:], ih_aggr(3))
+                + [then(forget(0, 0), hh_aggr(3), pool(gate_scales, 3)), REST, then(forget(0, 1), *pools(cell_sum, 0, (0, 1))), REST]
+                + chunks(ih_stat, 4) + [then(join(3, 0), ih_done(4), *pools(cell_sum, 0, (2, 3)))],
+                [REST] + square(4) + hh_with_bias(5, 3) + [then(hh(6, 0), hh_mean(5)), hh_square(5), REST],
+            ),
+            (
+                chunks(join, 3)[1:] + chunks(ih_stat, 5) + after_first(chunks(join, 4), ih_done(5)) + [c_stat(0, 0)],
+                [REST, REST] + pairs(3) + [then(hh(6, 1), mean_of_sum(4)), then(hh(6, 2), bias_of_gate(4)), hh(6, 3), hh_mean(6)] + tanh_pairs(1)[:2],
+            ),
+            (
+                chunks(c_stat, 0)[1:] + after_first(chunks(join, 5), c_aggr(0), pool(c_small, 0)) + chunks(ih_stat, 6),
+                [then(tanh_pairs(1)[2], mean_of_sum(5)), REST] + [then(hh_square(6), bias_of_gate(5)), REST, REST] + chunks(activate, 5) + [hh(7, 0), hh(7, 1)],
+            ),
+            (
+                [then(forget(1, 0), ih_done(6), *pools(cell_sum, 1, (0, 1))), REST, then(forget(1, 1), *pools(cell_sum, 1, (2, 3)), *pools(c_norm, 0, range(CHUNKS))), REST]
+                + chunks(ih_stat, 7) + after_first(chunks(c_stat, 1), ih_done(7))
+                + after_first(chunks(join, 6), c_aggr(1), pool(c_small, 1), *pools(c_norm, 1, range(CHUNKS))),
+                [then(hh(7, 2), mean_of_sum(6)), then(hh(7, 3), bias_of_gate(6)), hh_mean(7)] + square(7) + [REST] + weave(chunks(c_finish, 0), [REST] * 4),
+            ),
+            (
+                [join(7, 0), join(7, 1), REST, join(7, 2), h_finish(0, 0), join(7, 3), h_finish(0, 1), h_finish(1, 0), h_finish(0, 2), REST, h_finish(0, 3), h_finish(1, 1), REST, REST, h_finish(1, 2), REST, REST, h_finish(1, 3)],
+                [then(activate(6, 0, 2), mean_of_sum(7)), REST, then(activate(6, 2, 2), bias_of_gate(7)), c_finish(1, 0), activate(7, 0), REST, activate(7, 1), c_finish(1, 1), REST, activate(7, 2), c_finish(1, 2), REST, activate(7, 3), c_finish(1, 3)],
+            ),
+        ]
+
+
+        held = {}
+        used = [0, 0]
+        slots = []
+        for v, a in phases:
+            length = max(len(v), len(a))
+            slots.extend(zip(v + [REST] * (length - len(v)), a + [REST] * (length - len(a))))
+        for n in range(-LEAD, len(slots)):
+            for e in range(2):
+                if n + LEAD < len(slots) and slots[n + LEAD][e][0] is not None:
+                    held[(n + LEAD, e)] = slots[n + LEAD][e][0](e * BANKS + used[e] % BANKS)
+                    used[e] += 1
+            for e in range(2):
+                if n >= 0 and slots[n][e][1] is not None:
+                    slots[n][e][1](held.get((n, e)))

@@ -20,12 +20,15 @@ ROWS = B // P
 CHUNK = 512
 CHUNKS = B // CHUNK
 RPC = CHUNK // P
+PACK = 4
 F, IN, O, G = 0, 1, 2, 3
 TILES = [(IN, 0), (G, 0), (F, 0), (IN, 1), (G, 1), (F, 1), (O, 0), (O, 1)]
+FIRST_O = 6
+VECTOR_VAR = (0, 5)
 TINY = 2.0**-60
 BANKS = 4
 LEAD = 2
-VECTOR_VAR = (0, 3)
+G_HH, G_IH, BIAS, B_IH, B_HH, G_C, B_C, VEC_COLS = 0, 8, 16, 24, 32, 40, 42, 44
 
 
 def tile_lstmcell_kernel(
@@ -51,24 +54,25 @@ def tile_lstmcell_kernel(
         c_rows = tile("c_rows", [ROWS, H], BF16)
         wih_rows = tiles("wih_rows", 2, [4, I], BF16)
         whh_rows = tiles("whh_rows", 2, [4, H], BF16)
-        x_k = tiles("x_k", CHUNKS, [CHUNK, 4], BF16)
+        x_k = tiles("x_k", CHUNKS, [CHUNK, PACK], BF16)
         x_codes = tiles("x_codes", CHUNKS, [CHUNK], U32)
         x_scales = tiles("x_scales", CHUNKS, [CHUNK], U8)
-        wih_k = tiles("wih_k", 2, [4 * P, 4], BF16)
+        wih_k = tiles("wih_k", 2, [4 * P, PACK], BF16)
         wih_codes = tiles("wih_codes", 2, [4 * P], U32)
         wih_scales = tiles("wih_scales", 2, [4 * P], U8)
         h_t = tiles("h_t", CHUNKS, [2, CHUNK], BF16)
         whh_t = tiles("whh_t", 2, [4, 2, P], BF16)
         gate = tiles("gate", 8, [B], F32)
-        squares = tile("squares", [B], BF16)
+        squares = tiles("squares", 2, [B], BF16)
         c_out = tiles("c_out", 2 * CHUNKS, [RPC, P], F32)
         tanh_c = tiles("tanh_c", 2 * CHUNKS, [RPC, P], F32)
         h_out = tiles("h_out", CHUNKS, [RPC, H], F32)
         ident_f = tile("ident_f", [P], F32)
         ident_b = tile("ident_b", [P], BF16)
         vec_rows = tile("vec_rows", [P], BF16)
-        vec = tile("vec", [44], F32)
+        vec = tile("vec", [VEC_COLS], F32)
         powers = tile("powers", [3], F32)
+        eps = tile("eps", [1], F32)
         bias_sum = tile("bias_sum", [8], F32)
         nudge = tile("nudge", [8], F32)
         ghh_pm = tile("ghh_pm", [2, 8], F32)
@@ -81,7 +85,7 @@ def tile_lstmcell_kernel(
         hh_mv = tile("hh_mv", [8, 2], F32)
         var_eps = tile("var_eps", [8, 3], F32)
         roots = tile("roots", [8, 3], F32)
-        sum_mean = tile("sum_mean", [8], F32)
+        t_mean = tile("t_mean", [8], F32)
         hh_scale = tile("hh_scale", [8, 2], F32)
         ih_stats = tile("ih_stats", [8, CHUNKS, 6], F32)
         ih_mv = tile("ih_mv", [8, 2], F32)
@@ -107,23 +111,33 @@ def tile_lstmcell_kernel(
         def rows(k):
             return slice(k * RPC, (k + 1) * RPC)
 
-        def pool_tt(out, in0, in1, op):
-            nc.gpsimd.tensor_tensor(out=out, in0=in0, in1=in1, op=op)
+        def features(u):
+            return slice(u * P, (u + 1) * P)
 
-        def pool_affine(out, in0, scale, bias):
-            nc.gpsimd.tensor_scalar(out, in0, scale, bias, ALU.mult, ALU.add)
-
-        def pool_product(out, in0, a, b):
-            nc.gpsimd.tensor_scalar(out, in0, a, b, ALU.mult, ALU.mult)
+        def one(n):
+            return slice(n, n + 1)
 
         def column(t):
             return 2 * TILES[t][0] + TILES[t][1]
 
-        def one(t):
-            return slice(t, t + 1)
+        def cell_tile(u):
+            return gate[3 * u]
 
+        def gpsimd_tt(out, in0, in1, op):
+            nc.gpsimd.tensor_tensor(out=out, in0=in0, in1=in1, op=op)
+
+        def gpsimd_affine(out, in0, scale, bias):
+            nc.gpsimd.tensor_scalar(out, in0, scale, bias, ALU.mult, ALU.add)
+
+        def gpsimd_product(out, in0, first, second):
+            nc.gpsimd.tensor_scalar(out, in0, first, second, ALU.mult, ALU.mult)
+
+        def scalar_affine(out, in_, scale, bias):
+            nc.scalar.activation(out=out, in_=in_, func=ACT.Identity, scale=scale, bias=bias)
+
+        nc.sync.dma_start(out=h_rows[0][:], in_=h_v[:, rows(0), :])
         nc.sync.dma_start(out=whh_rows[0][:], in_=whh_v[0])
-        for k in range(CHUNKS):
+        for k in range(1, CHUNKS):
             nc.sync.dma_start(out=h_rows[k][:], in_=h_v[:, rows(k), :])
         nc.sync.dma_start(out=wih_rows[0][:], in_=wih_v[0])
         for k in range(CHUNKS):
@@ -137,6 +151,7 @@ def tile_lstmcell_kernel(
         nc.vector.memset(vec_rows[:], 0.0)
         nc.vector.memset(powers[:, 0:1], 0.5)
         nc.vector.memset(powers[:, 1:3], -0.5)
+        gpsimd_affine(eps[:], powers[:, 0:1], 0.0, EPS)
         row = 0
         for v in (g_hh, g_ih, b, b_ih, b_hh, g_c, b_c):
             count = v.shape[0] // P
@@ -145,6 +160,9 @@ def tile_lstmcell_kernel(
             )
             row += count
 
+        def no_bank(work, *args):
+            return None, lambda unused: work(*args)
+
         def vectors():
             def fill(n):
                 t = bank(n, [P], BF16)
@@ -152,28 +170,26 @@ def tile_lstmcell_kernel(
                 return t
 
             def read(t):
-                nc.vector.tensor_copy(out=vec[:], in_=t[:, 0:44])
-                pool_tt(nudge[:], vec[:, 0:8], vec[:, 0:8], ALU.mult)
+                nc.vector.tensor_copy(out=vec[:], in_=t[:, 0:VEC_COLS])
+                gain = vec[:, G_HH:G_IH]
+                gpsimd_tt(nudge[:], gain, gain, ALU.mult)
                 nc.gpsimd.tensor_scalar(
                     nudge[:], nudge[:], TINY * TINY, 2 * TINY, ALU.is_lt, ALU.mult
                 )
-                pool_tt(ghh_pm[:, 0, :], vec[:, 0:8], nudge[:], ALU.add)
-                pool_affine(ghh_pm[:, 1, :], ghh_pm[:, 0, :], -1.0, 0.0)
-                pool_affine(gc_pm[:, 0, :], vec[:, 40:42], 1.0, 0.0)
-                pool_affine(gc_pm[:, 1, :], vec[:, 40:42], -1.0, 0.0)
-                pool_tt(bias_sum[:], vec[:, 16:24], vec[:, 24:32], ALU.add)
-                pool_tt(bias_sum[:], bias_sum[:], vec[:, 32:40], ALU.add)
+                gpsimd_tt(ghh_pm[:, 0, :], gain, nudge[:], ALU.add)
+                gpsimd_affine(ghh_pm[:, 1, :], ghh_pm[:, 0, :], -1.0, 0.0)
+                gpsimd_affine(gc_pm[:, 0, :], vec[:, G_C:B_C], 1.0, 0.0)
+                gpsimd_affine(gc_pm[:, 1, :], vec[:, G_C:B_C], -1.0, 0.0)
+                gpsimd_tt(bias_sum[:], vec[:, BIAS:B_IH], vec[:, B_IH:B_HH], ALU.add)
+                gpsimd_tt(bias_sum[:], bias_sum[:], vec[:, B_HH:G_C], ALU.add)
 
             return fill, read
 
         def gain_ratio():
-            def read(t):
-                nc.vector.reciprocal(out=ghh_inv[:], in_=ghh_pm[:, 0, :])
-                pool_tt(g_ratio[:], vec[:, 8:16], ghh_inv[:], ALU.mult)
+            nc.vector.reciprocal(out=ghh_inv[:], in_=ghh_pm[:, 0, :])
+            gpsimd_tt(g_ratio[:], vec[:, G_IH:BIAS], ghh_inv[:], ALU.mult)
 
-            return None, read
-
-        def turn_whh(u, copy):
+        def turn_whh(u):
             def fill(n):
                 t = bank(n, [4, 2, P], BF16)
                 for g in range(4):
@@ -183,9 +199,9 @@ def tile_lstmcell_kernel(
                         )
                 return t
 
-            return fill, lambda t: copy(out=whh_t[u][:], in_=t[:])
+            return fill, lambda t: nc.scalar.copy(out=whh_t[u][:], in_=t[:])
 
-        def turn_h(k, copy):
+        def turn_h(k):
             def fill(n):
                 t = bank(n, [2, RPC, P], BF16)
                 for kc in range(2):
@@ -195,7 +211,10 @@ def tile_lstmcell_kernel(
                         )
                 return t
 
-            return fill, lambda t: copy(out=h_t[k][:], in_=t[:].rearrange("p a j n -> p a (j n)"))
+            def read(t):
+                nc.vector.tensor_copy(out=h_t[k][:], in_=t[:].rearrange("p a j n -> p a (j n)"))
+
+            return fill, read
 
         def turn_words(src, dst, pair, copy):
             def fill(n):
@@ -224,20 +243,17 @@ def tile_lstmcell_kernel(
             return turn_words(wih_rows[u], wih_k[u], pair, copy)
 
         def quantize(src, codes, scales):
-            def read(t):
-                nc.vector.quantize_mx(
-                    out=codes[:].bitcast(E5M2X4),
-                    scales=scales[:],
-                    in_=src[:].rearrange("p n j -> p (n j)"),
-                )
-
-            return None, read
+            nc.vector.quantize_mx(
+                out=codes[:].bitcast(E5M2X4),
+                scales=scales[:],
+                in_=src[:].rearrange("p n j -> p (n j)"),
+            )
 
         def quantize_x(k):
-            return quantize(x_k[k], x_codes[k], x_scales[k])
+            return no_bank(quantize, x_k[k], x_codes[k], x_scales[k])
 
         def quantize_wih(u):
-            return quantize(wih_k[u], wih_codes[u], wih_scales[u])
+            return no_bank(quantize, wih_k[u], wih_codes[u], wih_scales[u])
 
         def hh(t, k):
             g, u = TILES[t]
@@ -255,56 +271,45 @@ def tile_lstmcell_kernel(
                 return acc
 
             def read(acc):
-                nc.scalar.activation(
-                    out=gate[t][:, cols(k)],
-                    in_=acc[:],
-                    func=ACT.Identity,
-                    accum_out=hh_sums[:, t, k : k + 1],
-                )
+                if t in VECTOR_VAR:
+                    nc.scalar.copy(out=gate[t][:, cols(k)], in_=acc[:])
+                else:
+                    nc.scalar.activation(
+                        out=gate[t][:, cols(k)],
+                        in_=acc[:],
+                        func=ACT.Identity,
+                        accum_out=hh_sums[:, t, one(k)],
+                    )
 
-            def read_plain(acc):
-                nc.scalar.copy(out=gate[t][:, cols(k)], in_=acc[:])
+            return fill, read
 
-            return fill, read_plain if t in VECTOR_VAR else read
+        def aggregate(mv, stats, n):
+            nc.vector.bn_aggr(out=mv[:, n, :], in_=stats[:, n, :, :].rearrange("p k s -> p (k s)"))
 
         def hh_stat(t, k):
-            def read(unused):
-                nc.vector.bn_stats(out=hh_stats[:, t, k, :], in_=gate[t][:, cols(k)])
-
-            return None, read
+            return no_bank(nc.vector.bn_stats, hh_stats[:, t, k, :], gate[t][:, cols(k)])
 
         def hh_aggr(t):
-            def read(unused):
-                nc.vector.bn_aggr(
-                    out=hh_mv[:, t, :], in_=hh_stats[:, t, :, :].rearrange("p k s -> p (k s)")
-                )
-
-            return None, read
+            aggregate(hh_mv, hh_stats, t)
 
         def hh_mean(t):
-            def read(unused):
-                nc.scalar.activation(
-                    out=hh_parts[:, t, :],
-                    in_=hh_sums[:, t, :],
-                    func=ACT.Identity,
-                    scale=1.0 / B,
-                    accum_out=hh_mv[:, t, 0:1],
-                )
-
-            return None, read
+            nc.scalar.activation(
+                out=hh_parts[:, t, :],
+                in_=hh_sums[:, t, :],
+                func=ACT.Identity,
+                scale=1.0 / B,
+                accum_out=hh_mv[:, t, 0:1],
+            )
 
         def hh_square(t):
-            def read(unused):
-                nc.scalar.activation(
-                    out=squares[:],
-                    in_=gate[t][:],
-                    func=ACT.Square,
-                    scale=-1.0,
-                    bias=hh_mv[:, t, 0:1],
-                    accum_out=hh_mv[:, t, 1:2],
-                )
-
-            return None, read
+            nc.scalar.activation(
+                out=squares[t % 2][:],
+                in_=gate[t][:],
+                func=ACT.Square,
+                scale=-1.0,
+                bias=hh_mv[:, t, 0:1],
+                accum_out=hh_mv[:, t, 1:2],
+            )
 
         def ih_fill(t, k):
             g, u = TILES[t]
@@ -325,59 +330,52 @@ def tile_lstmcell_kernel(
             return fill
 
         def ih_stat(t, k):
-            def read(acc):
-                nc.vector.bn_stats(out=ih_stats[:, t, k, :], in_=acc[:])
-
-            return ih_fill(t, k), read
+            return ih_fill(t, k), lambda acc: nc.vector.bn_stats(ih_stats[:, t, k, :], acc[:])
 
         def ih_aggr(t):
-            def read(unused):
-                nc.vector.bn_aggr(
-                    out=ih_mv[:, t, :], in_=ih_stats[:, t, :, :].rearrange("p k s -> p (k s)")
-                )
+            aggregate(ih_mv, ih_stats, t)
 
-            return None, read
+        def hh_var_eps(t, affine=scalar_affine):
+            to_var = 1.0 if t in VECTOR_VAR else 1.0 / B
+            offset = eps[:] if affine is scalar_affine else EPS
+            affine(var_eps[:, t, 0:2], hh_mv[:, t, 1:2].to_broadcast([P, 2]), to_var, offset)
 
-        def gate_scales(t):
-            factor = 1.0 if t in VECTOR_VAR else 1.0 / B
-            pool_affine(var_eps[:, t, 0:2], hh_mv[:, t, 1:2].to_broadcast([P, 2]), factor, EPS)
-            pool_affine(var_eps[:, t, 2:3], ih_mv[:, t, 1:2], 1.0, EPS)
-            pool_tt(roots[:, t, :], var_eps[:, t, :], powers[:], ALU.pow)
-            pool_product(
+        def gate_ratio(t):
+            gpsimd_affine(var_eps[:, t, 2:3], ih_mv[:, t, 1:2], 1.0, EPS)
+            gpsimd_tt(roots[:, t, :], var_eps[:, t, :], powers[:], ALU.pow)
+            gpsimd_product(
                 ratio[:, one(t)], roots[:, t, 0:1], roots[:, t, 2:3], g_ratio[:, one(column(t))]
             )
-            pool_product(hh_scale[:, t, :], ghh_pm[:, :, column(t)], roots[:, t, 1:2], 1.0)
 
-        def mean_of_sum(t):
-            def read(unused):
-                nc.scalar.activation(
-                    out=sum_mean[:, one(t)],
-                    in_=ih_mv[:, t, 0:1],
-                    func=ACT.Identity,
-                    scale=ratio[:, one(t)],
-                    bias=hh_mv[:, t, 0:1],
-                )
+        def scale_and_mean(t, affine=scalar_affine):
+            affine(hh_scale[:, t, :], ghh_pm[:, :, column(t)], roots[:, t, 1:2], 0.0)
+            affine(t_mean[:, one(t)], ih_mv[:, t, 0:1], ratio[:, one(t)], hh_mv[:, t, 0:1])
 
-            return None, read
+        def bias_of_gate(t, affine=scalar_affine):
+            affine(
+                gate_bias[:, one(t)],
+                t_mean[:, one(t)],
+                hh_scale[:, t, 1:2],
+                bias_sum[:, one(column(t))],
+            )
 
-        def bias_of_gate(t):
-            def read(unused):
-                nc.scalar.activation(
-                    out=gate_bias[:, one(t)],
-                    in_=sum_mean[:, one(t)],
-                    func=ACT.Identity,
-                    scale=hh_scale[:, t, 1:2],
-                    bias=bias_sum[:, one(column(t))],
-                )
+        def factors_on_gpsimd(t):
+            ih_aggr(t)
+            hh_var_eps(t, gpsimd_affine)
+            gate_ratio(t)
+            scale_and_mean(t, gpsimd_affine)
+            bias_of_gate(t, gpsimd_affine)
 
-            return None, read
+        def ih_done(t):
+            ih_aggr(t)
+            gate_ratio(t)
 
         def join(t, k):
             def read(acc):
                 nc.vector.scalar_tensor_tensor(
                     out=gate[t][:, cols(k)],
                     in0=acc[:],
-                    scalar=ratio[:, t : t + 1],
+                    scalar=ratio[:, one(t)],
                     in1=gate[t][:, cols(k)],
                     op0=ALU.mult,
                     op1=ALU.add,
@@ -386,70 +384,59 @@ def tile_lstmcell_kernel(
             return ih_fill(t, k), read
 
         def activate(t, k, n=1):
-            g, u = TILES[t]
-
-            def read(unused):
+            def work():
                 nc.scalar.activation(
                     out=gate[t][:, cols(k, n)],
                     in_=gate[t][:, cols(k, n)],
-                    func=ACT.Tanh if g == G else ACT.Sigmoid,
+                    func=ACT.Tanh if TILES[t][0] == G else ACT.Sigmoid,
                     scale=hh_scale[:, t, 0:1],
-                    bias=gate_bias[:, t : t + 1],
+                    bias=gate_bias[:, one(t)],
                 )
 
-            return None, read
+            return no_bank(work)
 
-        def forget(u, half):
+        def input_gate(u, k, n):
+            cell = cell_tile(u)[:, cols(k, n)]
+            gpsimd_tt(cell, cell, gate[3 * u + 1][:, cols(k, n)], ALU.mult)
+
+        def forget(u, pair):
             def fill(n):
                 t = bank(n, [2 * RPC, P], BF16)
                 for j in range(2 * RPC):
-                    r = 2 * half * RPC + j
-                    nc.tensor.transpose(t[:, j, :], c_rows[:, r, u * P : (u + 1) * P], ident_b[:])
+                    r = 2 * pair * RPC + j
+                    nc.tensor.transpose(t[:, j, :], c_rows[:, r, features(u)], ident_b[:])
                 return t
 
             def read(t):
-                f = gate[3 * u + 2][:, cols(2 * half, 2)]
+                f = gate[3 * u + 2][:, cols(2 * pair, 2)]
                 nc.vector.tensor_tensor(
                     out=f, in0=t[:].rearrange("p j n -> p (j n)"), in1=f, op=ALU.mult
                 )
 
             return fill, read
 
+        def cell_sum(u, k, n):
+            cell = cell_tile(u)[:, cols(k, n)]
+            gpsimd_tt(cell, cell, gate[3 * u + 2][:, cols(k, n)], ALU.add)
+
         def c_stat(u, k):
-            def read(unused):
-                nc.vector.bn_stats(out=c_stats[:, u, k, :], in_=gate[3 * u][:, cols(k)])
+            return no_bank(nc.vector.bn_stats, c_stats[:, u, k, :], cell_tile(u)[:, cols(k)])
 
-            return None, read
+        def c_factors(u):
+            aggregate(c_mv, c_stats, u)
+            r = c_rstd[:, one(u)]
+            gpsimd_affine(r, c_mv[:, u, 1:2], 1.0, EPS)
+            gpsimd_tt(r, r, powers[:, 1:2], ALU.pow)
+            gpsimd_product(c_scale[:, u, :], gc_pm[:, :, u], r, 1.0)
+            gpsimd_affine(
+                c_bias[:, one(u)], c_mv[:, u, 0:1], c_scale[:, u, 1:2], vec[:, one(B_C + u)]
+            )
 
-        def c_aggr(u):
-            def read(unused):
-                nc.vector.bn_aggr(
-                    out=c_mv[:, u, :], in_=c_stats[:, u, :, :].rearrange("p k s -> p (k s)")
-                )
-
-            return None, read
-
-        def c_small(u):
-            r, bias = c_rstd[:, one(u)], c_bias[:, one(u)]
-            pool_affine(r, c_mv[:, u, 1:2], 1.0, EPS)
-            pool_tt(r, r, powers[:, 1:2], ALU.pow)
-            pool_product(c_scale[:, u, :], gc_pm[:, :, u], r, 1.0)
-            pool_affine(bias, c_mv[:, u, 0:1], c_scale[:, u, 1:2], vec[:, one(42 + u)])
-
-        def input_gate(u, k):
-            cell = gate[3 * u][:, cols(k)]
-            pool_tt(cell, cell, gate[3 * u + 1][:, cols(k)], ALU.mult)
-
-        def cell_sum(u, k):
-            cell = gate[3 * u][:, cols(k)]
-            pool_tt(cell, cell, gate[3 * u + 2][:, cols(k)], ALU.add)
-
-        def c_norm(u, k):
-            cell = gate[3 * u][:, cols(k)]
-            pool_affine(cell, cell, c_scale[:, u, 0:1], c_bias[:, one(u)])
-
-        def pool(work, *args):
-            return None, lambda unused: work(*args)
+        def c_norm(engine, u, k, n):
+            cell = cell_tile(u)[:, cols(k, n)]
+            engine.tensor_scalar(
+                cell, cell, c_scale[:, u, 0:1], c_bias[:, one(u)], ALU.mult, ALU.add
+            )
 
         def turn_back(src, k):
             def fill(n):
@@ -467,132 +454,155 @@ def tile_lstmcell_kernel(
             def read(t):
                 nc.scalar.activation(out=tanh_c[m][:], in_=t[:], func=ACT.Tanh)
                 nc.scalar.copy(out=c_out[m][:], in_=t[:])
-                nc.sync.dma_start(out=c_next_v[:, rows(k), u * P : (u + 1) * P], in_=c_out[m][:])
+                nc.sync.dma_start(out=c_next_v[:, rows(k), features(u)], in_=c_out[m][:])
 
-            return turn_back(gate[3 * u], k), read
+            return turn_back(cell_tile(u), k), read
 
         def h_finish(u, k):
-            m = u * CHUNKS + k
-
             def read(t):
                 nc.vector.tensor_tensor(
-                    out=h_out[k][:, :, u * P : (u + 1) * P],
+                    out=h_out[k][:, :, features(u)],
                     in0=t[:],
-                    in1=tanh_c[m][:],
+                    in1=tanh_c[u * CHUNKS + k][:],
                     op=ALU.mult,
                 )
                 if u == 1:
                     nc.sync.dma_start(out=h_next_v[:, rows(k), :], in_=h_out[k][:])
 
-            return turn_back(gate[6 + u], k), read
+            return turn_back(gate[FIRST_O + u], k), read
 
-        def chunks(step, *args):
-            return [step(*args, k) for k in range(CHUNKS)]
+        REST = (None, None)
 
-        def weave(*lists):
-            return [s for group in zip(*lists) for s in group]
-
-        def then(step, *more):
+        def then(step, *calls):
             def read(t):
                 step[1](t)
-                for extra in more:
-                    extra[1](None)
+                for work, *args in calls:
+                    work(*args)
 
             return step[0], read
 
-        def after_first(steps, *more):
-            return [then(steps[0], *more)] + steps[1:]
+        def chunks(step, n, first=0, last=CHUNKS):
+            return [step(n, k) for k in range(first, last)]
 
-        REST = (None, None)
+        def wide(t, k, *calls):
+            return [then(activate(t, k, 2), *calls), REST]
+
+        def square(t, *calls):
+            return [then(no_bank(hh_square, t), *calls), REST, REST, REST]
+
+        def spaced(steps):
+            return [entry for step in steps for entry in (step, REST)]
+
         v_copy, s_copy = nc.vector.tensor_copy, nc.scalar.copy
+        stages = []
 
+        stages.append((
+            [turn_h(0), turn_h(1), REST, turn_h(2), turn_h(3), turn_wih(0, 0, v_copy)]
+            + chunks(hh_stat, 0, 0, 2) + [quantize_wih(0)],
+            [turn_whh(0), REST, REST] + chunks(hh, 0, 0, 2) + [turn_wih(0, 1, s_copy)]
+            + chunks(hh, 0, 2) + [hh(1, 0)],
+        ))
+        between = [hh_stat(0, 2), hh_stat(0, 3), vectors()]
+        for k in range(CHUNKS - 1):
+            stages.append((
+                [turn_x(k, 0, v_copy), between[k], quantize_x(k)],
+                [turn_x(k, 1, s_copy), hh(1, k + 1)],
+            ))
+        last = CHUNKS - 1
+        stages.append((
+            [then(turn_x(last, 0, v_copy), (hh_aggr, 0)), ih_stat(0, 0), quantize_x(last)]
+            + [ih_stat(0, 1), then(ih_stat(0, 2), (gain_ratio,)), ih_stat(0, 3)]
+            + [then(ih_stat(1, 0), (factors_on_gpsimd, 0))] + chunks(ih_stat, 1, 1),
+            [then(turn_x(last, 1, s_copy), (hh_mean, 1)), REST] + square(1) + chunks(hh, 2),
+        ))
+        stages.append((
+            [then(join(0, 0), (factors_on_gpsimd, 1))] + chunks(join, 0, 1) + [ih_stat(2, 0)],
+            [then(turn_whh(1), (hh_mean, 2)), REST, activate(0, 0)] + square(2),
+        ))
+        stages.append((
+            chunks(ih_stat, 2, 1)
+            + [then(turn_wih(1, 0, v_copy), (factors_on_gpsimd, 2)), turn_wih(1, 1, v_copy)]
+            + [join(1, 0), quantize_wih(1), join(1, 1)],
+            chunks(hh, 3, 0, 2) + [activate(0, 1)] + chunks(hh, 3, 2) + wide(0, 2, (hh_mean, 3)),
+        ))
+        stages.append((
+            chunks(join, 1, 2) + chunks(join, 2) + chunks(ih_stat, 3, 0, 2),
+            wide(1, 0, (input_gate, 0, 0, 2)) + wide(1, 2, (input_gate, 0, 2, 2)) + square(3),
+        ))
+        stages.append((
+            chunks(ih_stat, 3, 2) + [then(ih_stat(4, 0), (ih_done, 3)), ih_stat(4, 1)]
+            + [then(forget(0, 0), (cell_sum, 0, 0, 2)), REST] + chunks(ih_stat, 4, 2),
+            [then(hh(4, 0), (hh_var_eps, 3)), activate(2, 0), activate(2, 1), hh(4, 1)]
+            + [activate(2, 2), hh(4, 2), activate(2, 3), then(hh(4, 3), (scale_and_mean, 3))],
+        ))
+        stages.append((
+            [then(forget(0, 1), (cell_sum, 0, 2, 2)), REST, then(join(3, 0), (ih_aggr, 4))]
+            + chunks(join, 3, 1) + chunks(c_stat, 0, 0, 2),
+            [then(hh(5, 0), (hh_mean, 4), (bias_of_gate, 3)), hh(5, 1)] + square(4)
+            + [then(hh(5, 2), (hh_var_eps, 4), (gate_ratio, 4)), hh(5, 3)],
+        ))
+        first_norm = [(c_factors, 0), (c_norm, nc.gpsimd, 0, 0, 2), (c_norm, nc.gpsimd, 0, 2, 2)]
+        stages.append((
+            chunks(c_stat, 0, 2) + [then(hh_stat(5, 0), *first_norm)] + chunks(hh_stat, 5, 1)
+            + [then(ih_stat(5, 0), (hh_aggr, 5)), ih_stat(5, 1)],
+            wide(3, 0) + wide(3, 2, (scale_and_mean, 4)) + [then(hh(6, 0), (bias_of_gate, 4))]
+            + chunks(hh, 6, 1, 3) + [then(hh(6, 3), (hh_var_eps, 5))],
+        ))
+        stages.append((
+            chunks(ih_stat, 5, 2) + [then(join(4, 0), (ih_done, 5))] + chunks(join, 4, 1)
+            + chunks(join, 5, 0, 2),
+            [then(hh(7, 0), (hh_mean, 6))] + chunks(hh, 7, 1, 3) + [REST]
+            + wide(4, 0, (input_gate, 1, 0, 2), (scale_and_mean, 5))
+            + wide(4, 2, (input_gate, 1, 2, 2), (bias_of_gate, 5)),
+        ))
+        stages.append((
+            chunks(join, 5, 2) + [ih_stat(6, 0)]
+            + [then(forget(1, 0), (cell_sum, 1, 0, 1), (cell_sum, 1, 1, 1)), REST]
+            + [then(forget(1, 1), (cell_sum, 1, 2, 1), (cell_sum, 1, 3, 1)), REST, ih_stat(6, 1)],
+            [hh(7, 3), activate(5, 0), then(activate(5, 1), (hh_mean, 7))]
+            + chunks(activate, 5, 2) + [no_bank(hh_square, 6)],
+        ))
+        stages.append((
+            chunks(ih_stat, 6, 2) + [then(ih_stat(7, 0), (ih_done, 6)), c_stat(1, 0)]
+            + [ih_stat(7, 1), c_stat(1, 1)] + chunks(ih_stat, 7, 2),
+            square(7, (hh_var_eps, 6))
+            + spaced([then(c_finish(0, 0), (hh_var_eps, 7)), c_finish(0, 1)]),
+        ))
+        stages.append((
+            [then(c_stat(1, 2), (ih_done, 7)), c_stat(1, 3), then(join(6, 0), (c_factors, 1))]
+            + chunks(join, 6, 1) + chunks(join, 7, 0, 2),
+            spaced([
+                then(c_finish(0, 2), (scale_and_mean, 6)),
+                then(c_finish(0, 3), (bias_of_gate, 6)),
+            ])
+            + wide(6, 0, (scale_and_mean, 7)) + wide(6, 2, (bias_of_gate, 7)),
+        ))
+        stages.append((
+            [no_bank(c_norm, nc.vector, 1, 0, 2), join(7, 2)]
+            + [no_bank(c_norm, nc.vector, 1, 2, 2), join(7, 3)]
+            + chunks(h_finish, 0, 0, 2) + [h_finish(1, 0)] + chunks(h_finish, 0, 2)
+            + spaced(chunks(h_finish, 1, 1)),
+            wide(7, 0) + [REST, c_finish(1, 0), REST] + wide(7, 2)
+            + spaced(chunks(c_finish, 1, 1)),
+        ))
 
-        def pairs(t):
-            return [activate(t, 0, 2), REST, activate(t, 2, 2), REST]
-
-        def square(t):
-            return [hh_square(t), REST, REST, REST]
-
-        def ih_done(t):
-            return then(ih_aggr(t), pool(gate_scales, t))
-
-        def pools(work, u, ks):
-            return [pool(work, u, k) for k in ks]
-
-        def hh_with_bias(t, earlier):
-            steps = chunks(hh, t)
-            return [then(steps[0], mean_of_sum(earlier)), then(steps[1], bias_of_gate(earlier))] + steps[2:]
-
-        def tanh_pairs(u):
-            t = 3 * u + 1
-            return [then(activate(t, 0, 2), *pools(input_gate, u, (0, 1))), REST, then(activate(t, 2, 2), *pools(input_gate, u, (2, 3))), REST]
-
-        head_vector = [
-            turn_whh(0, v_copy), turn_h(0, v_copy), turn_h(1, v_copy), turn_h(2, v_copy), turn_h(3, v_copy),
-            REST, turn_wih(0, 0, v_copy), hh_stat(0, 0), vectors(), quantize_wih(0),
-            turn_x(0, 0, v_copy), then(hh_stat(0, 1), gain_ratio()), quantize_x(0),
-            turn_x(1, 0, v_copy), hh_stat(0, 2), quantize_x(1),
-            turn_x(2, 0, v_copy), hh_stat(0, 3), quantize_x(2),
-            then(turn_x(3, 0, v_copy), hh_aggr(0)), ih_stat(0, 0), quantize_x(3),
-            ih_stat(0, 1), ih_stat(0, 2), ih_stat(0, 3),
-        ] + after_first(chunks(ih_stat, 1), ih_done(0))
-        head_scalar = [
-            REST, REST, REST, REST, hh(0, 0),
-            hh(0, 1), turn_wih(0, 1, s_copy), hh(0, 2), hh(0, 3), hh(1, 0),
-            turn_x(0, 1, s_copy), hh(1, 1), REST,
-            turn_x(1, 1, s_copy), hh(1, 2), REST,
-            turn_x(2, 1, s_copy), hh(1, 3), REST,
-            then(turn_x(3, 1, s_copy), hh_mean(1)), REST] + square(1) + chunks(hh, 2)
-        phases = [
-            (head_vector, head_scalar),
-            (
-                after_first(chunks(join, 0), ih_done(1)) + chunks(ih_stat, 2) + after_first(chunks(join, 1), ih_done(2)),
-                [then(turn_whh(1, s_copy), hh_mean(2), mean_of_sum(0))] + after_first(square(2), bias_of_gate(0))
-                + [then(activate(0, 0, 2), mean_of_sum(1)), REST, then(activate(0, 2, 2), bias_of_gate(1)), REST] + chunks(hh, 3)[:3],
-            ),
-            (
-                [turn_wih(1, 0, v_copy), turn_wih(1, 1, v_copy), join(2, 0), quantize_wih(1)] + chunks(join, 2)[1:]
-                + chunks(ih_stat, 3) + [hh_stat(3, 0)],
-                [hh(3, 3)] + tanh_pairs(0) + hh_with_bias(4, 2) + after_first(pairs(2), hh_mean(4))[:3],
-            ),
-            (
-                after_first(chunks(hh_stat, 3)[1:], ih_aggr(3))
-                + [then(forget(0, 0), hh_aggr(3), pool(gate_scales, 3)), REST, then(forget(0, 1), *pools(cell_sum, 0, (0, 1))), REST]
-                + chunks(ih_stat, 4) + [then(join(3, 0), ih_done(4), *pools(cell_sum, 0, (2, 3)))],
-                [REST] + square(4) + hh_with_bias(5, 3) + [then(hh(6, 0), hh_mean(5)), hh_square(5), REST],
-            ),
-            (
-                chunks(join, 3)[1:] + chunks(ih_stat, 5) + after_first(chunks(join, 4), ih_done(5)) + [c_stat(0, 0)],
-                [REST, REST] + pairs(3) + [then(hh(6, 1), mean_of_sum(4)), then(hh(6, 2), bias_of_gate(4)), hh(6, 3), hh_mean(6)] + tanh_pairs(1)[:2],
-            ),
-            (
-                chunks(c_stat, 0)[1:] + after_first(chunks(join, 5), c_aggr(0), pool(c_small, 0)) + chunks(ih_stat, 6),
-                [then(tanh_pairs(1)[2], mean_of_sum(5)), REST] + [then(hh_square(6), bias_of_gate(5)), REST, REST] + chunks(activate, 5) + [hh(7, 0), hh(7, 1)],
-            ),
-            (
-                [then(forget(1, 0), ih_done(6), *pools(cell_sum, 1, (0, 1))), REST, then(forget(1, 1), *pools(cell_sum, 1, (2, 3)), *pools(c_norm, 0, range(CHUNKS))), REST]
-                + chunks(ih_stat, 7) + after_first(chunks(c_stat, 1), ih_done(7))
-                + after_first(chunks(join, 6), c_aggr(1), pool(c_small, 1), *pools(c_norm, 1, range(CHUNKS))),
-                [then(hh(7, 2), mean_of_sum(6)), then(hh(7, 3), bias_of_gate(6)), hh_mean(7)] + square(7) + [REST] + weave(chunks(c_finish, 0), [REST] * 4),
-            ),
-            (
-                [join(7, 0), join(7, 1), REST, join(7, 2), h_finish(0, 0), join(7, 3), h_finish(0, 1), h_finish(1, 0), h_finish(0, 2), REST, h_finish(0, 3), h_finish(1, 1), REST, REST, h_finish(1, 2), REST, REST, h_finish(1, 3)],
-                [then(activate(6, 0, 2), mean_of_sum(7)), REST, then(activate(6, 2, 2), bias_of_gate(7)), c_finish(1, 0), activate(7, 0), REST, activate(7, 1), c_finish(1, 1), REST, activate(7, 2), c_finish(1, 2), REST, activate(7, 3), c_finish(1, 3)],
-            ),
-        ]
-
-
-        held = {}
+        entries = []
+        for on_vector, on_scalar in stages:
+            length = max(len(on_vector), len(on_scalar))
+            entries.extend(
+                zip(
+                    on_vector + [REST] * (length - len(on_vector)),
+                    on_scalar + [REST] * (length - len(on_scalar)),
+                )
+            )
+        filled = {}
         used = [0, 0]
-        slots = []
-        for v, a in phases:
-            length = max(len(v), len(a))
-            slots.extend(zip(v + [REST] * (length - len(v)), a + [REST] * (length - len(a))))
-        for n in range(-LEAD, len(slots)):
+        for n in range(-LEAD, len(entries)):
+            ahead = n + LEAD
             for e in range(2):
-                if n + LEAD < len(slots) and slots[n + LEAD][e][0] is not None:
-                    held[(n + LEAD, e)] = slots[n + LEAD][e][0](e * BANKS + used[e] % BANKS)
+                if ahead < len(entries) and entries[ahead][e][0] is not None:
+                    filled[(ahead, e)] = entries[ahead][e][0](e * BANKS + used[e] % BANKS)
                     used[e] += 1
             for e in range(2):
-                if n >= 0 and slots[n][e][1] is not None:
-                    slots[n][e][1](held.get((n, e)))
+                if n >= 0 and entries[n][e][1] is not None:
+                    entries[n][e][1](filled.get((n, e)))

@@ -28,6 +28,7 @@ VECTOR_VAR = (0, 5)
 TINY = 2.0**-60
 BANKS = 4
 LEAD = 2
+WARM_UPS = 4
 G_HH, G_IH, BIAS, B_IH, B_HH, G_C, B_C, VEC_COLS = 0, 8, 16, 24, 32, 40, 42, 44
 
 
@@ -145,6 +146,12 @@ def tile_lstmcell_kernel(
         nc.sync.dma_start(out=whh_rows[1][:], in_=whh_v[1])
         nc.sync.dma_start(out=wih_rows[1][:], in_=wih_v[1])
         nc.sync.dma_start(out=c_rows[:], in_=c_v)
+
+        warm = tile("warm", [CHUNK], BF16)
+        nc.vector.memset(warm[:], 0.0)
+        warm_out = bank(2 * BANKS - 1, [CHUNK], F32)
+        for n in range(WARM_UPS):
+            nc.tensor.matmul(out=warm_out[:], lhsT=warm[:, 0:P], rhs=warm[:], start=True, stop=True)
 
         make_identity(nc, ident_f[:])
         nc.scalar.activation(out=ident_b[:], in_=ident_f[:], func=ACT.Identity)

from contextlib import ExitStack

import concourse.mybir as mybir
from concourse.masks import make_identity

B, I, H = 2048, 512, 256
EPS = 1e-5
FLOPS = 2 * B * 4 * H * (I + H)

F32 = mybir.dt.float32
BF16 = mybir.dt.bfloat16
U32 = mybir.dt.uint32
U8 = mybir.dt.uint8
E5M2X4 = mybir.dt.float8_e5m2_x4
ALU = mybir.AluOpType
ACT = mybir.ActivationFunctionType

P = 128
ROWS = B // P
CHUNK = 512
CHUNKS = B // CHUNK
RPC = CHUNK // P
PACK = 4
F, IN, O, G = 0, 1, 2, 3
TILES = [(IN, 0), (G, 0), (F, 0), (IN, 1), (G, 1), (F, 1), (O, 0), (O, 1)]
FIRST_O = 6
VECTOR_VAR = (0, 5)
TINY = 2.0**-60
BANKS = 4
LEAD = 2
WARM_UPS = 4
G_HH, G_IH, BIAS, B_IH, B_HH, G_C, B_C, VEC_COLS = 0, 8, 16, 24, 32, 40, 42, 44


def tile_lstmcell_kernel(
    tc, x, c, h, w_ih, w_hh, b, g_ih, b_ih, g_hh, b_hh, g_c, b_c, out_0, out_1
):
    nc = tc.nc
    with ExitStack() as ctx:
        sb = ctx.enter_context(tc.tile_pool(name="sb", bufs=1))
        ps = ctx.enter_context(tc.psum_pool(name="ps", bufs=1))
        ctx.enter_context(tc.manual_schedule())

        def bank(n, shape, dtype):
            return ps.tile([P] + shape, dtype, name="bank%d" % n, tag="bank%d" % n)

        def tile(name, shape, dtype):
            return sb.tile([P] + shape, dtype, name=name, align_bytes=64)

        def tiles(name, count, shape, dtype):
            return [tile("%s%d" % (name, n), shape, dtype) for n in range(count)]

        x_rows = tiles("x_rows", CHUNKS, [RPC, I], BF16)
        h_rows = tiles("h_rows", CHUNKS, [RPC, H], BF16)
        c_rows = tile("c_rows", [ROWS, H], BF16)
        wih_rows = tiles("wih_rows", 2, [4, I], BF16)
        whh_rows = tiles("whh_rows", 2, [4, H], BF16)
        x_k = tiles("x_k", CHUNKS, [CHUNK, PACK], BF16)
        x_codes = tiles("x_codes", CHUNKS, [CHUNK], U32)
        x_scales = tiles("x_scales", CHUNKS, [CHUNK], U8)
        wih_k = tiles("wih_k", 2, [4 * P, PACK], BF16)
        wih_codes = tiles("wih_codes", 2, [4 * P], U32)
        wih_scales = tiles("wih_scales", 2, [4 * P], U8)
        h_t = tiles("h_t", CHUNKS, [2, CHUNK], BF16)
        whh_t = tiles("whh_t", 2, [4, 2, P], BF16)
        gate = tiles("gate", 8, [B], F32)
        squares = tiles("squares", 2, [B], BF16)
        c_out = tiles("c_out", 2 * CHUNKS, [RPC, P], F32)
        tanh_c = tiles("tanh_c", 2 * CHUNKS, [RPC, P], F32)
        h_out = tiles("h_out", CHUNKS, [RPC, H], F32)
        ident_f = tile("ident_f", [P], F32)
        ident_b = tile("ident_b", [P], BF16)
        vec_rows = tile("vec_rows", [P], BF16)
        vec = tile("vec", [VEC_COLS], F32)
        powers = tile("powers", [3], F32)
        eps = tile("eps", [1], F32)
        bias_sum = tile("bias_sum", [8], F32)
        nudge = tile("nudge", [8], F32)
        ghh_pm = tile("ghh_pm", [2, 8], F32)
        gc_pm = tile("gc_pm", [2, 2], F32)
        ghh_inv = tile("ghh_inv", [8], F32)
        g_ratio = tile("g_ratio", [8], F32)
        hh_sums = tile("hh_sums", [8, CHUNKS], F32)
        hh_parts = tile("hh_parts", [8, CHUNKS], F32)
        hh_stats = tile("hh_stats", [8, CHUNKS, 6], F32)
        hh_mv = tile("hh_mv", [8, 2], F32)
        var_eps = tile("var_eps", [8, 3], F32)
        roots = tile("roots", [8, 3], F32)
        t_mean = tile("t_mean", [8], F32)
        hh_scale = tile("hh_scale", [8, 2], F32)
        ih_stats = tile("ih_stats", [8, CHUNKS, 6], F32)
        ih_mv = tile("ih_mv", [8, 2], F32)
        ratio = tile("ratio", [8], F32)
        gate_bias = tile("gate_bias", [8], F32)
        c_stats = tile("c_stats", [2, CHUNKS, 6], F32)
        c_mv = tile("c_mv", [2, 2], F32)
        c_scale = tile("c_scale", [2, 2], F32)
        c_rstd = tile("c_rstd", [2], F32)
        c_bias = tile("c_bias", [2], F32)

        x_v = x.rearrange("(p r) k -> p r k", r=ROWS)
        h_v = h.rearrange("(p r) k -> p r k", r=ROWS)
        c_v = c.rearrange("(p r) k -> p r k", r=ROWS)
        wih_v = w_ih.rearrange("(g u m) k -> u m g k", g=4, u=2)
        whh_v = w_hh.rearrange("(g u m) k -> u m g k", g=4, u=2)
        c_next_v = out_0.rearrange("(p r) f -> p r f", r=ROWS)
        h_next_v = out_1.rearrange("(p r) f -> p r f", r=ROWS)

        def cols(k, n=1):
            return slice(k * CHUNK, (k + n) * CHUNK)

        def rows(k):
            return slice(k * RPC, (k + 1) * RPC)

        def features(u):
            return slice(u * P, (u + 1) * P)

        def one(n):
            return slice(n, n + 1)

        def column(t):
            return 2 * TILES[t][0] + TILES[t][1]

        def cell_tile(u):
            return gate[3 * u]

        def gpsimd_tt(out, in0, in1, op):
            nc.gpsimd.tensor_tensor(out=out, in0=in0, in1=in1, op=op)

        def gpsimd_affine(out, in0, scale, bias):
            nc.gpsimd.tensor_scalar(out, in0, scale, bias, ALU.mult, ALU.add)

        def gpsimd_product(out, in0, first, second):
            nc.gpsimd.tensor_scalar(out, in0, first, second, ALU.mult, ALU.mult)

        def scalar_affine(out, in_, scale, bias):
            nc.scalar.activation(out=out, in_=in_, func=ACT.Identity, scale=scale, bias=bias)

        nc.sync.dma_start(out=h_rows[0][:], in_=h_v[:, rows(0), :])
        nc.sync.dma_start(out=whh_rows[0][:], in_=whh_v[0])
        for k in range(1, CHUNKS):
            nc.sync.dma_start(out=h_rows[k][:], in_=h_v[:, rows(k), :])
        nc.sync.dma_start(out=wih_rows[0][:], in_=wih_v[0])
        for k in range(CHUNKS):
            nc.sync.dma_start(out=x_rows[k][:], in_=x_v[:, rows(k), :])
        nc.sync.dma_start(out=whh_rows[1][:], in_=whh_v[1])
        nc.sync.dma_start(out=wih_rows[1][:], in_=wih_v[1])
        nc.sync.dma_start(out=c_rows[:], in_=c_v)

        warm = tile("warm", [CHUNK], BF16)
        nc.vector.memset(warm[:], 0.0)
        warm_out = bank(2 * BANKS - 1, [CHUNK], F32)
        for n in range(WARM_UPS):
            nc.tensor.matmul(out=warm_out[:], lhsT=warm[:, 0:P], rhs=warm[:], start=True, stop=True)

        make_identity(nc, ident_f[:])
        nc.scalar.activation(out=ident_b[:], in_=ident_f[:], func=ACT.Identity)
        nc.vector.memset(vec_rows[:], 0.0)
        nc.vector.memset(powers[:, 0:1], 0.5)
        nc.vector.memset(powers[:, 1:3], -0.5)
        gpsimd_affine(eps[:], powers[:, 0:1], 0.0, EPS)
        row = 0
        for v in (g_hh, g_ih, b, b_ih, b_hh, g_c, b_c):
            count = v.shape[0] // P
            nc.gpsimd.dma_start(
                out=vec_rows[row : row + count, :], in_=v.rearrange("(t m) -> t m", m=P)
            )
            row += count

        def no_bank(work, *args):
            return None, lambda unused: work(*args)

        def vectors():
            def fill(n):
                t = bank(n, [P], BF16)
                nc.tensor.transpose(t[:], vec_rows[:], ident_b[:])
                return t

            def read(t):
                nc.vector.tensor_copy(out=vec[:], in_=t[:, 0:VEC_COLS])
                gain = vec[:, G_HH:G_IH]
                gpsimd_tt(nudge[:], gain, gain, ALU.mult)
                nc.gpsimd.tensor_scalar(
                    nudge[:], nudge[:], TINY * TINY, 2 * TINY, ALU.is_lt, ALU.mult
                )
                gpsimd_tt(ghh_pm[:, 0, :], gain, nudge[:], ALU.add)
                gpsimd_affine(ghh_pm[:, 1, :], ghh_pm[:, 0, :], -1.0, 0.0)
                gpsimd_affine(gc_pm[:, 0, :], vec[:, G_C:B_C], 1.0, 0.0)
                gpsimd_affine(gc_pm[:, 1, :], vec[:, G_C:B_C], -1.0, 0.0)
                gpsimd_tt(bias_sum[:], vec[:, BIAS:B_IH], vec[:, B_IH:B_HH], ALU.add)
                gpsimd_tt(bias_sum[:], bias_sum[:], vec[:, B_HH:G_C], ALU.add)

            return fill, read

        def gain_ratio():
            nc.vector.reciprocal(out=ghh_inv[:], in_=ghh_pm[:, 0, :])
            gpsimd_tt(g_ratio[:], vec[:, G_IH:BIAS], ghh_inv[:], ALU.mult)

        def turn_whh(u):
            def fill(n):
                t = bank(n, [4, 2, P], BF16)
                for g in range(4):
                    for kc in range(2):
                        nc.tensor.transpose(
                            t[:, g, kc, :], whh_rows[u][:, g, kc * P : (kc + 1) * P], ident_b[:]
                        )
                return t

            return fill, lambda t: nc.scalar.copy(out=whh_t[u][:], in_=t[:])

        def turn_h(k):
            def fill(n):
                t = bank(n, [2, RPC, P], BF16)
                for kc in range(2):
                    for j in range(RPC):
                        nc.tensor.transpose(
                            t[:, kc, j, :], h_rows[k][:, j, kc * P : (kc + 1) * P], ident_b[:]
                        )
                return t

            def read(t):
                nc.vector.tensor_copy(out=h_t[k][:], in_=t[:].rearrange("p a j n -> p a (j n)"))

            return fill, read

        def turn_words(src, dst, pair, copy):
            def fill(n):
                words = src[:].bitcast(F32)
                t = bank(n, [2, 2, P], F32)
                for j in range(2):
                    for w in range(2):
                        nc.tensor.transpose(
                            t[:, j, w, :], words[:, 2 * pair + j, w : I // 2 : 2], ident_f[:]
                        )
                return t

            def read(t):
                out = dst[:, 2 * pair * P : 2 * (pair + 1) * P, :].bitcast(F32)
                copy(
                    out=out.rearrange("p (j n) w -> p j n w", j=2),
                    in_=t[:].rearrange("p j w n -> p j n w"),
                )

            return fill, read

        def turn_x(k, pair, copy):
            return turn_words(x_rows[k], x_k[k], pair, copy)

        def turn_wih(u, pair, copy):
            return turn_words(wih_rows[u], wih_k[u], pair, copy)

        def quantize(src, codes, scales):
            nc.vector.quantize_mx(
                out=codes[:].bitcast(E5M2X4),
                scales=scales[:],
                in_=src[:].rearrange("p n j -> p (n j)"),
            )

        def quantize_x(k):
            return no_bank(quantize, x_k[k], x_codes[k], x_scales[k])

        def quantize_wih(u):
            return no_bank(quantize, wih_k[u], wih_codes[u], wih_scales[u])

        def hh(t, k):
            g, u = TILES[t]

            def fill(n):
                acc = bank(n, [CHUNK], F32)
                for kc in range(2):
                    nc.tensor.matmul(
                        out=acc[:],
                        lhsT=whh_t[u][:, g, kc, :],
                        rhs=h_t[k][:, kc, :],
                        start=(kc == 0),
                        stop=(kc == 1),
                    )
                return acc

            def read(acc):
                if t in VECTOR_VAR:
                    nc.scalar.copy(out=gate[t][:, cols(k)], in_=acc[:])
                else:
                    nc.scalar.activation(
                        out=gate[t][:, cols(k)],
                        in_=acc[:],
                        func=ACT.Identity,
                        accum_out=hh_sums[:, t, one(k)],
                    )

            return fill, read

        def aggregate(mv, stats, n):
            nc.vector.bn_aggr(out=mv[:, n, :], in_=stats[:, n, :, :].rearrange("p k s -> p (k s)"))

        def hh_stat(t, k):
            return no_bank(nc.vector.bn_stats, hh_stats[:, t, k, :], gate[t][:, cols(k)])

        def hh_aggr(t):
            aggregate(hh_mv, hh_stats, t)

        def hh_mean(t):
            nc.scalar.activation(
                out=hh_parts[:, t, :],
                in_=hh_sums[:, t, :],
                func=ACT.Identity,
                scale=1.0 / B,
                accum_out=hh_mv[:, t, 0:1],
            )

        def hh_square(t):
            nc.scalar.activation(
                out=squares[t % 2][:],
                in_=gate[t][:],
                func=ACT.Square,
                scale=-1.0,
                bias=hh_mv[:, t, 0:1],
                accum_out=hh_mv[:, t, 1:2],
            )

        def ih_fill(t, k):
            g, u = TILES[t]

            def fill(n):
                acc = bank(n, [CHUNK], F32)
                nc.tensor.matmul_mx(
                    out=acc[:],
                    lhsT=wih_codes[u][:, g * P : (g + 1) * P].bitcast(E5M2X4),
                    lhsT_scale=wih_scales[u][:, g * P : (g + 1) * P],
                    rhs=x_codes[k][:].bitcast(E5M2X4),
                    rhs_scale=x_scales[k][:],
                    start=True,
                    stop=True,
                )
                return acc

            return fill

        def ih_stat(t, k):
            return ih_fill(t, k), lambda acc: nc.vector.bn_stats(ih_stats[:, t, k, :], acc[:])

        def ih_aggr(t):
            aggregate(ih_mv, ih_stats, t)

        def hh_var_eps(t, affine=scalar_affine):
            to_var = 1.0 if t in VECTOR_VAR else 1.0 / B
            offset = eps[:] if affine is scalar_affine else EPS
            affine(var_eps[:, t, 0:2], hh_mv[:, t, 1:2].to_broadcast([P, 2]), to_var, offset)

        def gate_ratio(t):
            gpsimd_affine(var_eps[:, t, 2:3], ih_mv[:, t, 1:2], 1.0, EPS)
            gpsimd_tt(roots[:, t, :], var_eps[:, t, :], powers[:], ALU.pow)
            gpsimd_product(
                ratio[:, one(t)], roots[:, t, 0:1], roots[:, t, 2:3], g_ratio[:, one(column(t))]
            )

        def scale_and_mean(t, affine=scalar_affine):
            affine(hh_scale[:, t, :], ghh_pm[:, :, column(t)], roots[:, t, 1:2], 0.0)
            affine(t_mean[:, one(t)], ih_mv[:, t, 0:1], ratio[:, one(t)], hh_mv[:, t, 0:1])

        def bias_of_gate(t, affine=scalar_affine):
            affine(
                gate_bias[:, one(t)],
                t_mean[:, one(t)],
                hh_scale[:, t, 1:2],
                bias_sum[:, one(column(t))],
            )

        def factors_on_gpsimd(t):
            ih_aggr(t)
            hh_var_eps(t, gpsimd_affine)
            gate_ratio(t)
            scale_and_mean(t, gpsimd_affine)
            bias_of_gate(t, gpsimd_affine)

        def ih_done(t):
            ih_aggr(t)
            gate_ratio(t)

        def join(t, k):
            def read(acc):
                nc.vector.scalar_tensor_tensor(
                    out=gate[t][:, cols(k)],
                    in0=acc[:],
                    scalar=ratio[:, one(t)],
                    in1=gate[t][:, cols(k)],
                    op0=ALU.mult,
                    op1=ALU.add,
                )

            return ih_fill(t, k), read

        def activate(t, k, n=1):
            def work():
                nc.scalar.activation(
                    out=gate[t][:, cols(k, n)],
                    in_=gate[t][:, cols(k, n)],
                    func=ACT.Tanh if TILES[t][0] == G else ACT.Sigmoid,
                    scale=hh_scale[:, t, 0:1],
                    bias=gate_bias[:, one(t)],
                )

            return no_bank(work)

        def input_gate(u, k, n):
            cell = cell_tile(u)[:, cols(k, n)]
            gpsimd_tt(cell, cell, gate[3 * u + 1][:, cols(k, n)], ALU.mult)

        def forget(u, pair):
            def fill(n):
                t = bank(n, [2 * RPC, P], BF16)
                for j in range(2 * RPC):
                    r = 2 * pair * RPC + j
                    nc.tensor.transpose(t[:, j, :], c_rows[:, r, features(u)], ident_b[:])
                return t

            def read(t):
                f = gate[3 * u + 2][:, cols(2 * pair, 2)]
                nc.vector.tensor_tensor(
                    out=f, in0=t[:].rearrange("p j n -> p (j n)"), in1=f, op=ALU.mult
                )

            return fill, read

        def cell_sum(u, k, n):
            cell = cell_tile(u)[:, cols(k, n)]
            gpsimd_tt(cell, cell, gate[3 * u + 2][:, cols(k, n)], ALU.add)

        def c_stat(u, k):
            return no_bank(nc.vector.bn_stats, c_stats[:, u, k, :], cell_tile(u)[:, cols(k)])

        def c_factors(u):
            aggregate(c_mv, c_stats, u)
            r = c_rstd[:, one(u)]
            gpsimd_affine(r, c_mv[:, u, 1:2], 1.0, EPS)
            gpsimd_tt(r, r, powers[:, 1:2], ALU.pow)
            gpsimd_product(c_scale[:, u, :], gc_pm[:, :, u], r, 1.0)
            gpsimd_affine(
                c_bias[:, one(u)], c_mv[:, u, 0:1], c_scale[:, u, 1:2], vec[:, one(B_C + u)]
            )

        def c_norm(engine, u, k, n):
            cell = cell_tile(u)[:, cols(k, n)]
            engine.tensor_scalar(
                cell, cell, c_scale[:, u, 0:1], c_bias[:, one(u)], ALU.mult, ALU.add
            )

        def turn_back(src, k):
            def fill(n):
                t = bank(n, [RPC, P], F32)
                for j in range(RPC):
                    r = k * RPC + j
                    nc.tensor.transpose(t[:, j, :], src[:, r * P : (r + 1) * P], ident_f[:])
                return t

            return fill

        def c_finish(u, k):
            m = u * CHUNKS + k

            def read(t):
                nc.scalar.activation(out=tanh_c[m][:], in_=t[:], func=ACT.Tanh)
                nc.scalar.copy(out=c_out[m][:], in_=t[:])
                nc.sync.dma_start(out=c_next_v[:, rows(k), features(u)], in_=c_out[m][:])

            return turn_back(cell_tile(u), k), read

        def h_finish(u, k):
            def read(t):
                nc.vector.tensor_tensor(
                    out=h_out[k][:, :, features(u)],
                    in0=t[:],
                    in1=tanh_c[u * CHUNKS + k][:],
                    op=ALU.mult,
                )
                if u == 1:
                    nc.sync.dma_start(out=h_next_v[:, rows(k), :], in_=h_out[k][:])

            return turn_back(gate[FIRST_O + u], k), read

        REST = (None, None)

        def then(step, *calls):
            def read(t):
                step[1](t)
                for work, *args in calls:
                    work(*args)

            return step[0], read

        def chunks(step, n, first=0, last=CHUNKS):
            return [step(n, k) for k in range(first, last)]

        def wide(t, k, *calls):
            return [then(activate(t, k, 2), *calls), REST]

        def square(t, *calls):
            return [then(no_bank(hh_square, t), *calls), REST, REST, REST]

        def spaced(steps):
            return [entry for step in steps for entry in (step, REST)]

        v_copy, s_copy = nc.vector.tensor_copy, nc.scalar.copy
        stages = []

        stages.append((
            [turn_h(0), turn_h(1), REST, turn_h(2), turn_h(3), turn_wih(0, 0, v_copy)]
            + chunks(hh_stat, 0, 0, 2) + [quantize_wih(0)],
            [turn_whh(0), REST, REST] + chunks(hh, 0, 0, 2) + [turn_wih(0, 1, s_copy)]
            + chunks(hh, 0, 2) + [hh(1, 0)],
        ))
        between = [hh_stat(0, 2), hh_stat(0, 3), vectors()]
        for k in range(CHUNKS - 1):
            stages.append((
                [turn_x(k, 0, v_copy), between[k], quantize_x(k)],
                [turn_x(k, 1, s_copy), hh(1, k + 1)],
            ))
        last = CHUNKS - 1
        stages.append((
            [then(turn_x(last, 0, v_copy), (hh_aggr, 0)), ih_stat(0, 0), quantize_x(last)]
            + [ih_stat(0, 1), then(ih_stat(0, 2), (gain_ratio,)), ih_stat(0, 3)]
            + [then(ih_stat(1, 0), (factors_on_gpsimd, 0))] + chunks(ih_stat, 1, 1),
            [then(turn_x(last, 1, s_copy), (hh_mean, 1)), REST] + square(1) + chunks(hh, 2),
        ))
        stages.append((
            [then(join(0, 0), (factors_on_gpsimd, 1))] + chunks(join, 0, 1) + [ih_stat(2, 0)],
            [then(turn_whh(1), (hh_mean, 2)), REST, activate(0, 0)] + square(2),
        ))
        stages.append((
            chunks(ih_stat, 2, 1)
            + [then(turn_wih(1, 0, v_copy), (factors_on_gpsimd, 2)), turn_wih(1, 1, v_copy)]
            + [join(1, 0), quantize_wih(1), join(1, 1)],
            chunks(hh, 3, 0, 2) + [activate(0, 1)] + chunks(hh, 3, 2) + wide(0, 2, (hh_mean, 3)),
        ))
        stages.append((
            chunks(join, 1, 2) + chunks(join, 2) + chunks(ih_stat, 3, 0, 2),
            wide(1, 0, (input_gate, 0, 0, 2)) + wide(1, 2, (input_gate, 0, 2, 2)) + square(3),
        ))
        stages.append((
            chunks(ih_stat, 3, 2) + [then(ih_stat(4, 0), (ih_done, 3)), ih_stat(4, 1)]
            + [then(forget(0, 0), (cell_sum, 0, 0, 2)), REST] + chunks(ih_stat, 4, 2),
            [then(hh(4, 0), (hh_var_eps, 3)), activate(2, 0), activate(2, 1), hh(4, 1)]
            + [activate(2, 2), hh(4, 2), activate(2, 3), then(hh(4, 3), (scale_and_mean, 3))],
        ))
        stages.append((
            [then(forget(0, 1), (cell_sum, 0, 2, 2)), REST, then(join(3, 0), (ih_aggr, 4))]
            + chunks(join, 3, 1) + chunks(c_stat, 0, 0, 2),
            [then(hh(5, 0), (hh_mean, 4), (bias_of_gate, 3)), hh(5, 1)] + square(4)
            + [then(hh(5, 2), (hh_var_eps, 4), (gate_ratio, 4)), hh(5, 3)],
        ))
        first_norm = [(c_factors, 0), (c_norm, nc.gpsimd, 0, 0, 2), (c_norm, nc.gpsimd, 0, 2, 2)]
        stages.append((
            chunks(c_stat, 0, 2) + [then(hh_stat(5, 0), *first_norm)] + chunks(hh_stat, 5, 1)
            + [then(ih_stat(5, 0), (hh_aggr, 5)), ih_stat(5, 1)],
            wide(3, 0) + wide(3, 2, (scale_and_mean, 4)) + [then(hh(6, 0), (bias_of_gate, 4))]
            + chunks(hh, 6, 1, 3) + [then(hh(6, 3), (hh_var_eps, 5))],
        ))
        stages.append((
            chunks(ih_stat, 5, 2) + [then(join(4, 0), (ih_done, 5))] + chunks(join, 4, 1)
            + chunks(join, 5, 0, 2),
            [then(hh(7, 0), (hh_mean, 6))] + chunks(hh, 7, 1, 3) + [REST]
            + wide(4, 0, (input_gate, 1, 0, 2), (scale_and_mean, 5))
            + wide(4, 2, (input_gate, 1, 2, 2), (bias_of_gate, 5)),
        ))
        stages.append((
            chunks(join, 5, 2) + [ih_stat(6, 0)]
            + [then(forget(1, 0), (cell_sum, 1, 0, 1), (cell_sum, 1, 1, 1)), REST]
            + [then(forget(1, 1), (cell_sum, 1, 2, 1), (cell_sum, 1, 3, 1)), REST, ih_stat(6, 1)],
            [hh(7, 3), activate(5, 0), then(activate(5, 1), (hh_mean, 7))]
            + chunks(activate, 5, 2) + [no_bank(hh_square, 6)],
        ))
        stages.append((
            chunks(ih_stat, 6, 2) + [then(ih_stat(7, 0), (ih_done, 6)), c_stat(1, 0)]
            + [ih_stat(7, 1), c_stat(1, 1)] + chunks(ih_stat, 7, 2),
            square(7, (hh_var_eps, 6))
            + spaced([then(c_finish(0, 0), (hh_var_eps, 7)), c_finish(0, 1)]),
        ))
        stages.append((
            [then(c_stat(1, 2), (ih_done, 7)), c_stat(1, 3), then(join(6, 0), (c_factors, 1))]
            + chunks(join, 6, 1) + chunks(join, 7, 0, 2),
            spaced([
                then(c_finish(0, 2), (scale_and_mean, 6)),
                then(c_finish(0, 3), (bias_of_gate, 6)),
            ])
            + wide(6, 0, (scale_and_mean, 7)) + wide(6, 2, (bias_of_gate, 7)),
        ))
        stages.append((
            [no_bank(c_norm, nc.vector, 1, 0, 2), join(7, 2)]
            + [no_bank(c_norm, nc.vector, 1, 2, 2), join(7, 3)]
            + chunks(h_finish, 0, 0, 2) + [h_finish(1, 0)] + chunks(h_finish, 0, 2)
            + spaced(chunks(h_finish, 1, 1)),
            wide(7, 0) + [REST, c_finish(1, 0), REST] + wide(7, 2)
            + spaced(chunks(c_finish, 1, 1)),
        ))

        entries = []
        for on_vector, on_scalar in stages:
            length = max(len(on_vector), len(on_scalar))
            entries.extend(
                zip(
                    on_vector + [REST] * (length - len(on_vector)),
                    on_scalar + [REST] * (length - len(on_scalar)),
                )
            )
        filled = {}
        used = [0, 0]
        for n in range(-LEAD, len(entries)):
            ahead = n + LEAD
            for e in range(2):
                if ahead < len(entries) and entries[ahead][e][0] is not None:
                    filled[(ahead, e)] = entries[ahead][e][0](e * BANKS + used[e] % BANKS)
                    used[e] += 1
            for e in range(2):
                if n >= 0 and entries[n][e][1] is not None:
                    entries[n][e][1](filled.get((n, e)))
